import numpy as np
import ml_dtypes


def mxq(x, axis, fmt="e4m3"):
    dtype, down = {"e4m3": (ml_dtypes.float8_e4m3fn, 7), "e5m2": (ml_dtypes.float8_e5m2, 14)}[fmt]
    v = np.moveaxis(np.asarray(x, np.float32).astype(ml_dtypes.bfloat16).astype(np.float64), axis, -1)
    blocks = v.reshape(v.shape[:-1] + (-1, 32))
    amax = np.abs(blocks).max(-1, keepdims=True)
    byte = np.maximum(np.where(amax > 0, np.frexp(amax)[1] - 1 + 127, 0) - down, 1)
    scale = np.exp2(byte - 127.0)
    codes = (blocks / scale).astype(np.float32).astype(dtype).astype(np.float64)
    return np.moveaxis((codes * scale).reshape(v.shape), -1, axis)


WIDE = False


def mx_kscale(k):
    if not WIDE:
        return np.ones(k)
    levels = np.array([10, -10, 5, -5, 0])
    a = np.random.permutation(np.resize(levels, k // 512 * 4)).reshape(k // 512, 4)
    idx = np.arange(k)
    return np.exp2(a[idx // 512, idx % 128 // 32])


BF16 = ml_dtypes.bfloat16


def bf(x):
    return np.asarray(x, np.float32).astype(BF16)


def f64(x):
    return np.asarray(x).astype(np.float64)


E2M1 = np.array([0.0, 0.5, 1.0, 1.5, 2.0, 3.0, 4.0, 6.0, -0.0, -0.5, -1.0, -1.5, -2.0, -3.0, -4.0, -6.0])


def pack_weight(w, fmt):
    k, n = w.shape
    w = f64(bf(w)).reshape(k // 32, 32, n)
    amax = np.abs(w).max(1)
    if fmt == "e4m3":
        byte = np.frexp(amax)[1] - 1 + 127 - 7
    else:
        mant, ex = np.frexp(amax / 6.0)
        byte = np.where(mant > 0.5, ex, ex - 1) + 127
    byte = np.clip(np.where(amax > 0, byte, 1), 1, 254)
    scaled = (w * np.exp2(127.0 - byte)[:, None, :]).reshape(k, n).astype(np.float32)
    by_word = np.ascontiguousarray(scaled.reshape(k // 512, 128, 4, n).transpose(0, 1, 3, 2))
    if fmt == "e4m3":
        words = by_word.astype(ml_dtypes.float8_e4m3fn).view(np.uint8)
    else:
        c = by_word.astype(ml_dtypes.float4_e2m1fn).view(np.uint8) & 0xF
        words = c[..., 0::2] | (c[..., 1::2] << 4)
    return np.ascontiguousarray(words), np.ascontiguousarray(byte.astype(np.uint8).reshape(k // 512, 16, n))


def unpack_weight(words, scales, fmt):
    g, p, n, _ = words.shape
    if fmt == "e4m3":
        vals = np.ascontiguousarray(words).view(ml_dtypes.float8_e4m3fn).astype(np.float64)
    else:
        nib = np.empty((g, p, n, 4), np.uint8)
        nib[..., 0::2] = words & 0xF
        nib[..., 1::2] = words >> 4
        vals = E2M1[nib]
    vals = vals * np.repeat(np.exp2(scales.astype(np.float64) - 127.0), 8, axis=1)[..., None]
    return vals.transpose(0, 1, 3, 2).reshape(g * 512, n)


B, N, D, H, DH = 4, 128, 16384, 16, 64
R = 2 * DH
EPS = 1e-12
BASE = 10000.0
FMT = "e4m3"


def l2norm(t):
    n = np.sqrt(np.sum(t * t, axis=-1, keepdims=True))
    return t / np.maximum(n, EPS)


def rotate_half(t):
    t1, t2 = np.split(t, 2, axis=-1)
    return np.concatenate([-t2, t1], axis=-1)


def rope_tables():
    inv_freq = 1.0 / (BASE ** (np.arange(0, R, 2) / R))
    freqs = np.outer(np.arange(N), inv_freq)
    emb = np.concatenate([freqs, freqs], axis=-1)
    return np.cos(emb), np.sin(emb)


def setup_inputs():
    s, t = mx_kscale(D), mx_kscale(D)
    g = np.sqrt(DH)
    x = bf(np.random.standard_normal((B, N, D)) * s)
    a = bf(np.random.standard_normal((B, N, D)) * t)
    wx_words, wx_scales = pack_weight((np.random.standard_normal((R, D)) / np.sqrt(D) / s).T, FMT)
    wa_words, wa_scales = pack_weight((np.random.standard_normal((R, D)) / np.sqrt(D) / t).T, FMT)
    kx_scale = bf(g * (1.0 + 0.1 * np.random.standard_normal((1, 1, DH))))
    ka_scale = bf(g * (1.0 + 0.1 * np.random.standard_normal((1, 1, DH))))
    return {
        "x": x,
        "a": a,
        "Wkv_x_words": wx_words,
        "Wkv_x_scales": wx_scales,
        "Wkv_a_words": wa_words,
        "Wkv_a_scales": wa_scales,
        "kx_scale": kx_scale,
        "ka_scale": ka_scale,
    }


def reference(x, a, Wkv_x_words, Wkv_x_scales, Wkv_a_words, Wkv_a_scales, kx_scale, ka_scale):
    kv_x = mxq(f64(x), 2, "e4m3") @ unpack_weight(Wkv_x_words, Wkv_x_scales, FMT)
    kv_a = mxq(f64(a), 2, "e4m3") @ unpack_weight(Wkv_a_words, Wkv_a_scales, FMT)
    k_x, v_x = np.split(kv_x[:, None], 2, axis=-1)
    k_a, v_a = np.split(kv_a[:, None], 2, axis=-1)
    k_x = l2norm(k_x) * f64(kx_scale)
    k_a = l2norm(k_a) * f64(ka_scale)
    k = np.concatenate([k_x, k_a], axis=-1)
    v = np.concatenate([v_x, v_a], axis=-1)
    cos, sin = rope_tables()
    k = k * cos + rotate_half(k) * sin
    return k[:, 0], v[:, 0]

@@ -1,0 +1,255 @@
+import math
+from contextlib import ExitStack
+
+import concourse.mybir as mybir
+from concourse.masks import make_identity
+
+F32 = mybir.dt.float32
+BF16 = mybir.dt.bfloat16
+I32 = mybir.dt.int32
+U32 = mybir.dt.uint32
+U8 = mybir.dt.uint8
+FP8X4 = mybir.dt.float8_e4m3fn_x4
+ALU = mybir.AluOpType
+ACT = mybir.ActivationFunctionType
+
+P = 128
+BATCHES = 4
+D = 16384
+DH = 64
+STREAMS = 2
+EPS = 1e-12
+ROPE_BASE = 10000.0
+
+K_PASS = 4 * P
+PASSES = D // K_PASS
+PAIRS_PER_PASS = K_PASS // 2
+PASSES_PER_CHUNK = 8
+CHUNK_COLS = PASSES_PER_CHUNK * K_PASS
+CHUNKS_PER_ROW = PASSES // PASSES_PER_CHUNK
+PASSES_PER_BANK = 2
+BANKS_PER_CHUNK = PASSES_PER_CHUNK // PASSES_PER_BANK
+X_BUFFERS = 8
+
+FLOPS = 2 * STREAMS * BATCHES * P * D * P
+
+
+def tile_cmattention_pb_k_kernel(
+    tc, x, a, wx_words, wx_scales, wa_words, wa_scales, kx_scale, ka_scale, k_out, v_out
+):
+    nc = tc.nc
+    acts = (x, a)
+    words_in = (wx_words, wa_words)
+    scales_in = (wx_scales, wa_scales)
+    gains_in = (kx_scale, ka_scale)
+
+    chunks = [
+        (s, b, c)
+        for s in range(STREAMS)
+        for b in range(BATCHES)
+        for c in range(CHUNKS_PER_ROW)
+    ]
+
+    with ExitStack() as ctx:
+        ctx.enter_context(tc.manual_schedule())
+        const = ctx.enter_context(tc.tile_pool(name="const", bufs=1))
+        x_pool = ctx.enter_context(tc.tile_pool(name="x_pool", bufs=X_BUFFERS))
+        mx_pool = ctx.enter_context(tc.tile_pool(name="mx_pool", bufs=3))
+        small = ctx.enter_context(tc.tile_pool(name="small", bufs=2))
+        psum_t = ctx.enter_context(tc.psum_pool(name="psum_t", bufs=6))
+        psum_acc = ctx.enter_context(tc.psum_pool(name="psum_acc", bufs=2))
+
+        w_words = [
+            const.tile([P, PASSES, P], U32, name="w_words%d" % s, align_bytes=64)
+            for s in range(STREAMS)
+        ]
+        w_scales = [
+            const.tile([P, PASSES, P], U8, name="w_scales%d" % s, align_bytes=64)
+            for s in range(STREAMS)
+        ]
+        for s in range(STREAMS):
+            nc.vector.memset(w_scales[s][:].bitcast(I32), 0)
+
+        def load_weight_scales(s):
+            for q in range(4):
+                nc.sync.dma_start(
+                    out=w_scales[s][32 * q : 32 * q + 4].bitcast(I32),
+                    in_=scales_in[s][:, 4 * q : 4 * q + 4, :]
+                    .rearrange("g r n -> r g n")
+                    .bitcast(I32),
+                )
+
+        def load_weight_words(s, c):
+            passes = slice(c * PASSES_PER_CHUNK, (c + 1) * PASSES_PER_CHUNK)
+            nc.sync.dma_start(
+                out=w_words[s][:, passes, :].bitcast(I32),
+                in_=words_in[s][passes].rearrange("g p n t -> p g (n t)").bitcast(I32),
+            )
+
+        x_tiles = []
+
+        def load_chunk(i):
+            s, b, c = chunks[i]
+            x_sb = x_pool.tile([P, CHUNK_COLS], BF16, name="x_sb")
+            nc.sync.dma_start(
+                out=x_sb[:], in_=acts[s][b, :, c * CHUNK_COLS : (c + 1) * CHUNK_COLS]
+            )
+            x_tiles.append(x_sb)
+            if b == 0:
+                load_weight_words(s, c)
+                if c == 0:
+                    load_weight_scales(s)
+
+        for i in range(X_BUFFERS - 1):
+            load_chunk(i)
+
+        gains = const.tile([P, STREAMS, DH], BF16, name="gains")
+        for s in range(STREAMS):
+            nc.scalar.dma_start(
+                out=gains[:, s, :],
+                in_=gains_in[s].rearrange("a b d -> (a b d)").partition_broadcast(P),
+            )
+
+        ident = const.tile([P, P], F32, name="ident")
+        make_identity(nc, ident[:])
+
+        turn_offsets = ((0.25, 0.0), (0.5, 0.25))
+        col_i = const.tile([P, DH], I32, name="col_i")
+        nc.gpsimd.iota(col_i[:], pattern=[[1, DH]], base=0, channel_multiplier=0)
+        pos_i = const.tile([P, 1], I32, name="pos_i")
+        nc.gpsimd.iota(pos_i[:], pattern=[[0, 1]], base=0, channel_multiplier=1)
+        minus_half = const.tile([P, 1], F32, name="minus_half")
+        nc.gpsimd.memset(minus_half[:], -0.5)
+
+        col_f = const.tile([P, DH], F32, name="col_f")
+        nc.vector.tensor_copy(out=col_f[:], in_=col_i[:])
+        pos_turns = const.tile([P, 1], F32, name="pos_turns")
+        nc.vector.tensor_scalar_mul(out=pos_turns[:], in0=pos_i[:], scalar1=0.5 / math.pi)
+        freq = const.tile([P, DH], F32, name="freq")
+        nc.scalar.activation(
+            out=freq[:], in_=col_f[:], func=ACT.Exp, scale=-math.log(ROPE_BASE) / DH
+        )
+        turns = const.tile([P, STREAMS, 2, DH], F32, name="turns")
+        for s in range(STREAMS):
+            for h in range(2):
+                nc.vector.tensor_scalar(
+                    out=turns[:, s, h, :],
+                    in0=freq[:],
+                    scalar1=pos_turns[:, 0:1],
+                    scalar2=turn_offsets[s][h],
+                    op0=ALU.mult,
+                    op1=ALU.add,
+                )
+        flat = "p s h j -> p (s h j)"
+        whole_i = const.tile([P, STREAMS, 2, DH], I32, name="whole_i")
+        nc.vector.tensor_copy(out=whole_i[:], in_=turns[:])
+        whole_f = const.tile([P, STREAMS, 2, DH], F32, name="whole_f")
+        nc.vector.tensor_copy(out=whole_f[:], in_=whole_i[:])
+        left = const.tile([P, STREAMS, 2, DH], F32, name="left")
+        nc.vector.tensor_sub(out=left[:], in0=turns[:], in1=whole_f[:])
+        minus_turn = const.tile([P, STREAMS, 2, DH], F32, name="minus_turn")
+        nc.vector.scalar_tensor_tensor(
+            out=minus_turn[:].rearrange(flat),
+            in0=left[:].rearrange(flat),
+            scalar=0.5,
+            in1=left[:].rearrange(flat),
+            op0=ALU.is_gt,
+            op1=ALU.subtract,
+        )
+        trig = const.tile([P, STREAMS, 2, DH], F32, name="trig")
+        nc.scalar.activation(
+            out=trig[:], in_=minus_turn[:], func=ACT.Sin, scale=-2.0 * math.pi
+        )
+        table = const.tile([P, STREAMS, 2, DH], F32, name="table")
+        nc.vector.tensor_tensor(
+            out=table[:],
+            in0=trig[:],
+            in1=gains[:].unsqueeze(2).to_broadcast([P, STREAMS, 2, DH]),
+            op=ALU.mult,
+        )
+
+        k_from_x = [const.tile([P, 2, DH], F32, name="k_from_x%d" % b) for b in range(BATCHES)]
+        v_sb = [const.tile([P, STREAMS, DH], F32, name="v_sb%d" % b) for b in range(BATCHES)]
+
+        def transpose_and_quantise(i):
+            pairs = x_tiles[i][:].bitcast(F32)
+            grouped = mx_pool.tile([P, CHUNK_COLS], BF16, name="grouped", align_bytes=64)
+            grouped_pairs = grouped[:].bitcast(F32).rearrange("p (g r u) -> p g r u", r=P, u=2)
+            for h in range(BANKS_PER_CHUNK):
+                bank = psum_t.tile([P, PASSES_PER_BANK, 2, P], F32, name="bank")
+                for j in range(PASSES_PER_BANK):
+                    first = (h * PASSES_PER_BANK + j) * PAIRS_PER_PASS
+                    for u in range(2):
+                        nc.tensor.transpose(
+                            bank[:, j, u, :],
+                            pairs[:, first + u : first + PAIRS_PER_PASS : 2],
+                            ident[:],
+                        )
+                copy_out = nc.vector.tensor_copy if h == 0 else nc.scalar.copy
+                copy_out(
+                    out=grouped_pairs[:, h * PASSES_PER_BANK : (h + 1) * PASSES_PER_BANK],
+                    in_=bank[:].rearrange("p j u r -> p j r u"),
+                )
+            codes = mx_pool.tile([P, PASSES_PER_CHUNK * P], U32, name="codes", align_bytes=64)
+            scales = mx_pool.tile([P, PASSES_PER_CHUNK * P], U8, name="scales", align_bytes=64)
+            nc.vector.quantize_mx(out=codes[:].bitcast(FP8X4), scales=scales[:], in_=grouped[:])
+            return codes, scales
+
+        def multiply(i, codes, scales, acc):
+            s, b, c = chunks[i]
+            for j in range(PASSES_PER_CHUNK):
+                g = c * PASSES_PER_CHUNK + j
+                tokens = slice(j * P, (j + 1) * P)
+                nc.tensor.matmul_mx(
+                    out=acc[:],
+                    lhsT=codes[:, tokens].bitcast(FP8X4),
+                    lhsT_scale=scales[:, tokens],
+                    rhs=w_words[s][:, g, :].bitcast(FP8X4),
+                    rhs_scale=w_scales[s][:, g, :],
+                    start=(g == 0),
+                    stop=(g == PASSES - 1),
+                )
+
+        def finish(s, b, acc):
+            nc.scalar.copy(out=v_sb[b][:, s, :], in_=acc[:, DH : 2 * DH])
+            squares = small.tile([P, DH], F32, name="squares")
+            sum_sq = small.tile([P, 1], F32, name="sum_sq")
+            nc.scalar.activation(
+                out=squares[:], in_=acc[:, 0:DH], func=ACT.Square, accum_out=sum_sq[:]
+            )
+            floored = small.tile([P, 1], F32, name="floored")
+            nc.gpsimd.tensor_scalar_max(out=floored[:], in0=sum_sq[:], scalar1=EPS * EPS)
+            inv_norm = small.tile([P, 1], F32, name="inv_norm")
+            nc.gpsimd.tensor_tensor(
+                out=inv_norm[:], in0=floored[:], in1=minus_half[:], op=ALU.pow
+            )
+            share = k_from_x[b] if s == 0 else small.tile([P, 2, DH], F32, name="k_from_a")
+            nc.vector.scalar_tensor_tensor(
+                out=share[:],
+                in0=acc[:, 0:DH].unsqueeze(1).to_broadcast([P, 2, DH]),
+                scalar=inv_norm[:, 0:1],
+                in1=table[:, s],
+                op0=ALU.mult,
+                op1=ALU.mult,
+            )
+            if s == STREAMS - 1:
+                k_sb = small.tile([P, 2, DH], F32, name="k_sb")
+                nc.vector.tensor_add(out=k_sb[:], in0=k_from_x[b][:], in1=share[:])
+                nc.sync.dma_start(out=k_out[b], in_=k_sb[:].rearrange("p h j -> p (h j)"))
+                nc.sync.dma_start(out=v_out[b], in_=v_sb[b][:].rearrange("p s j -> p (s j)"))
+
+        quantised = []
+        acc = None
+        for i in range(len(chunks) + 1):
+            if i + X_BUFFERS - 1 < len(chunks):
+                load_chunk(i + X_BUFFERS - 1)
+            if i < len(chunks):
+                quantised.append(transpose_and_quantise(i))
+            if i >= 1:
+                s, b, c = chunks[i - 1]
+                if c == 0:
+                    acc = psum_acc.tile([P, P], F32, name="acc")
+                codes, scales = quantised[i - 1]
+                multiply(i - 1, codes, scales, acc)
+                if c == CHUNKS_PER_ROW - 1:
+                    finish(s, b, acc)

@@ -23,7 +23,6 @@ ROPE_BASE = 10000.0
 
 K_PASS = 4 * P
 PASSES = D // K_PASS
-PAIRS_PER_PASS = K_PASS // 2
 PASSES_PER_CHUNK = 8
 CHUNK_COLS = PASSES_PER_CHUNK * K_PASS
 CHUNKS_PER_ROW = PASSES // PASSES_PER_CHUNK
@@ -54,6 +53,7 @@ def tile_cmattention_pb_k_kernel(
         ctx.enter_context(tc.manual_schedule())
         const = ctx.enter_context(tc.tile_pool(name="const", bufs=1))
         x_pool = ctx.enter_context(tc.tile_pool(name="x_pool", bufs=X_BUFFERS))
+        sort_pool = ctx.enter_context(tc.tile_pool(name="sort_pool", bufs=3))
         mx_pool = ctx.enter_context(tc.tile_pool(name="mx_pool", bufs=3))
         small = ctx.enter_context(tc.tile_pool(name="small", bufs=2))
         psum_t = ctx.enter_context(tc.psum_pool(name="psum_t", bufs=6))
@@ -171,22 +171,30 @@ def tile_cmattention_pb_k_kernel(
         k_from_x = [const.tile([P, 2, DH], F32, name="k_from_x%d" % b) for b in range(BATCHES)]
         v_sb = [const.tile([P, STREAMS, DH], F32, name="v_sb%d" % b) for b in range(BATCHES)]
 
+        sorted_tiles = []
+
+        def sort_pairs(i):
+            sorted_pairs = sort_pool.tile([P, PASSES_PER_CHUNK, 2, P], F32, name="sorted_pairs")
+            nc.vector.tensor_copy(
+                out=sorted_pairs[:],
+                in_=x_tiles[i][:].bitcast(F32).rearrange("p (g q u) -> p g u q", q=P, u=2),
+            )
+            sorted_tiles.append(sorted_pairs)
+
         def transpose_and_quantise(i):
-            pairs = x_tiles[i][:].bitcast(F32)
+            sorted_pairs = sorted_tiles[i]
             grouped = mx_pool.tile([P, CHUNK_COLS], BF16, name="grouped", align_bytes=64)
             grouped_pairs = grouped[:].bitcast(F32).rearrange("p (g r u) -> p g r u", r=P, u=2)
             for h in range(BANKS_PER_CHUNK):
                 bank = psum_t.tile([P, PASSES_PER_BANK, 2, P], F32, name="bank")
                 for j in range(PASSES_PER_BANK):
-                    first = (h * PASSES_PER_BANK + j) * PAIRS_PER_PASS
                     for u in range(2):
                         nc.tensor.transpose(
                             bank[:, j, u, :],
-                            pairs[:, first + u : first + PAIRS_PER_PASS : 2],
+                            sorted_pairs[:, h * PASSES_PER_BANK + j, u, :],
                             ident[:],
                         )
-                copy_out = nc.vector.tensor_copy if h == 0 else nc.scalar.copy
-                copy_out(
+                nc.scalar.copy(
                     out=grouped_pairs[:, h * PASSES_PER_BANK : (h + 1) * PASSES_PER_BANK],
                     in_=bank[:].rearrange("p j u r -> p j r u"),
                 )
@@ -240,9 +248,12 @@ def tile_cmattention_pb_k_kernel(
 
         quantised = []
         acc = None
+        sort_pairs(0)
         for i in range(len(chunks) + 1):
             if i + X_BUFFERS - 1 < len(chunks):
                 load_chunk(i + X_BUFFERS - 1)
+            if i + 1 < len(chunks):
+                sort_pairs(i + 1)
             if i < len(chunks):
                 quantised.append(transpose_and_quantise(i))
             if i >= 1:

@@ -23,9 +23,13 @@ ROPE_BASE = 10000.0
 
 K_PASS = 4 * P
 PASSES = D // K_PASS
+PAIRS_PER_PASS = K_PASS // 2
 PASSES_PER_CHUNK = 8
 CHUNK_COLS = PASSES_PER_CHUNK * K_PASS
-CHUNKS_PER_ROW = PASSES // PASSES_PER_CHUNK
+PASSES_PER_GROUP = 16
+GROUPS_PER_STREAM = PASSES // PASSES_PER_GROUP
+CHUNKS_PER_BATCH = PASSES_PER_GROUP // PASSES_PER_CHUNK
+CHUNKS_PER_GROUP = BATCHES * CHUNKS_PER_BATCH
 PASSES_PER_BANK = 2
 BANKS_PER_CHUNK = PASSES_PER_CHUNK // PASSES_PER_BANK
 X_BUFFERS = 8
@@ -43,21 +47,22 @@ def tile_cmattention_pb_k_kernel(
     gains_in = (kx_scale, ka_scale)
 
     chunks = [
-        (s, b, c)
+        (s, g, b, c)
         for s in range(STREAMS)
+        for g in range(GROUPS_PER_STREAM)
         for b in range(BATCHES)
-        for c in range(CHUNKS_PER_ROW)
+        for c in range(CHUNKS_PER_BATCH)
     ]
 
     with ExitStack() as ctx:
         ctx.enter_context(tc.manual_schedule())
         const = ctx.enter_context(tc.tile_pool(name="const", bufs=1))
         x_pool = ctx.enter_context(tc.tile_pool(name="x_pool", bufs=X_BUFFERS))
-        sort_pool = ctx.enter_context(tc.tile_pool(name="sort_pool", bufs=3))
-        mx_pool = ctx.enter_context(tc.tile_pool(name="mx_pool", bufs=3))
+        stage = ctx.enter_context(tc.tile_pool(name="stage", bufs=3))
+        mx_pool = ctx.enter_context(tc.tile_pool(name="mx_pool", bufs=CHUNKS_PER_GROUP))
         small = ctx.enter_context(tc.tile_pool(name="small", bufs=2))
-        psum_t = ctx.enter_context(tc.psum_pool(name="psum_t", bufs=6))
-        psum_acc = ctx.enter_context(tc.psum_pool(name="psum_acc", bufs=2))
+        psum_t = ctx.enter_context(tc.psum_pool(name="psum_t", bufs=4))
+        psum_acc = ctx.enter_context(tc.psum_pool(name="psum_acc", bufs=BATCHES))
 
         w_words = [
             const.tile([P, PASSES, P], U32, name="w_words%d" % s, align_bytes=64)
@@ -79,8 +84,8 @@ def tile_cmattention_pb_k_kernel(
                     .bitcast(I32),
                 )
 
-        def load_weight_words(s, c):
-            passes = slice(c * PASSES_PER_CHUNK, (c + 1) * PASSES_PER_CHUNK)
+        def load_weight_words(s, g):
+            passes = slice(g * PASSES_PER_GROUP, (g + 1) * PASSES_PER_GROUP)
             nc.sync.dma_start(
                 out=w_words[s][:, passes, :].bitcast(I32),
                 in_=words_in[s][passes].rearrange("g p n t -> p g (n t)").bitcast(I32),
@@ -89,16 +94,15 @@ def tile_cmattention_pb_k_kernel(
         x_tiles = []
 
         def load_chunk(i):
-            s, b, c = chunks[i]
+            s, g, b, c = chunks[i]
+            first_col = (g * CHUNKS_PER_BATCH + c) * CHUNK_COLS
             x_sb = x_pool.tile([P, CHUNK_COLS], BF16, name="x_sb")
-            nc.sync.dma_start(
-                out=x_sb[:], in_=acts[s][b, :, c * CHUNK_COLS : (c + 1) * CHUNK_COLS]
-            )
+            nc.sync.dma_start(out=x_sb[:], in_=acts[s][b, :, first_col : first_col + CHUNK_COLS])
             x_tiles.append(x_sb)
-            if b == 0:
-                load_weight_words(s, c)
-                if c == 0:
+            if (i + 1) % CHUNKS_PER_GROUP == 0:
+                if g == 0:
                     load_weight_scales(s)
+                load_weight_words(s, g)
 
         for i in range(X_BUFFERS - 1):
             load_chunk(i)
@@ -171,51 +175,46 @@ def tile_cmattention_pb_k_kernel(
         k_from_x = [const.tile([P, 2, DH], F32, name="k_from_x%d" % b) for b in range(BATCHES)]
         v_sb = [const.tile([P, STREAMS, DH], F32, name="v_sb%d" % b) for b in range(BATCHES)]
 
-        sorted_tiles = []
-
-        def sort_pairs(i):
-            sorted_pairs = sort_pool.tile([P, PASSES_PER_CHUNK, 2, P], F32, name="sorted_pairs")
-            nc.vector.tensor_copy(
-                out=sorted_pairs[:],
-                in_=x_tiles[i][:].bitcast(F32).rearrange("p (g q u) -> p g u q", q=P, u=2),
-            )
-            sorted_tiles.append(sorted_pairs)
-
-        def transpose_and_quantise(i):
-            sorted_pairs = sorted_tiles[i]
-            grouped = mx_pool.tile([P, CHUNK_COLS], BF16, name="grouped", align_bytes=64)
+        def transpose(i):
+            pairs = x_tiles[i][:].bitcast(F32)
+            grouped = stage.tile([P, CHUNK_COLS], BF16, name="grouped", align_bytes=64)
             grouped_pairs = grouped[:].bitcast(F32).rearrange("p (g r u) -> p g r u", r=P, u=2)
             for h in range(BANKS_PER_CHUNK):
                 bank = psum_t.tile([P, PASSES_PER_BANK, 2, P], F32, name="bank")
                 for j in range(PASSES_PER_BANK):
+                    first = (h * PASSES_PER_BANK + j) * PAIRS_PER_PASS
                     for u in range(2):
                         nc.tensor.transpose(
                             bank[:, j, u, :],
-                            sorted_pairs[:, h * PASSES_PER_BANK + j, u, :],
+                            pairs[:, first + u : first + PAIRS_PER_PASS : 2],
                             ident[:],
                         )
-                nc.scalar.copy(
+                copy_out = nc.vector.tensor_copy if h == 0 else nc.scalar.copy
+                copy_out(
                     out=grouped_pairs[:, h * PASSES_PER_BANK : (h + 1) * PASSES_PER_BANK],
                     in_=bank[:].rearrange("p j u r -> p j r u"),
                 )
+            return grouped
+
+        def quantise(grouped):
             codes = mx_pool.tile([P, PASSES_PER_CHUNK * P], U32, name="codes", align_bytes=64)
             scales = mx_pool.tile([P, PASSES_PER_CHUNK * P], U8, name="scales", align_bytes=64)
             nc.vector.quantize_mx(out=codes[:].bitcast(FP8X4), scales=scales[:], in_=grouped[:])
             return codes, scales
 
         def multiply(i, codes, scales, acc):
-            s, b, c = chunks[i]
+            s, g, b, c = chunks[i]
             for j in range(PASSES_PER_CHUNK):
-                g = c * PASSES_PER_CHUNK + j
+                k_pass = g * PASSES_PER_GROUP + c * PASSES_PER_CHUNK + j
                 tokens = slice(j * P, (j + 1) * P)
                 nc.tensor.matmul_mx(
                     out=acc[:],
                     lhsT=codes[:, tokens].bitcast(FP8X4),
                     lhsT_scale=scales[:, tokens],
-                    rhs=w_words[s][:, g, :].bitcast(FP8X4),
-                    rhs_scale=w_scales[s][:, g, :],
-                    start=(g == 0),
-                    stop=(g == PASSES - 1),
+                    rhs=w_words[s][:, k_pass, :].bitcast(FP8X4),
+                    rhs_scale=w_scales[s][:, k_pass, :],
+                    start=(k_pass == 0),
+                    stop=(k_pass == PASSES - 1),
                 )
 
         def finish(s, b, acc):
@@ -243,24 +242,27 @@ def tile_cmattention_pb_k_kernel(
             if s == STREAMS - 1:
                 k_sb = small.tile([P, 2, DH], F32, name="k_sb")
                 nc.vector.tensor_add(out=k_sb[:], in0=k_from_x[b][:], in1=share[:])
-                nc.sync.dma_start(out=k_out[b], in_=k_sb[:].rearrange("p h j -> p (h j)"))
                 nc.sync.dma_start(out=v_out[b], in_=v_sb[b][:].rearrange("p s j -> p (s j)"))
+                nc.sync.dma_start(out=k_out[b], in_=k_sb[:].rearrange("p h j -> p (h j)"))
 
-        quantised = []
-        acc = None
-        sort_pairs(0)
-        for i in range(len(chunks) + 1):
-            if i + X_BUFFERS - 1 < len(chunks):
-                load_chunk(i + X_BUFFERS - 1)
-            if i + 1 < len(chunks):
-                sort_pairs(i + 1)
-            if i < len(chunks):
-                quantised.append(transpose_and_quantise(i))
-            if i >= 1:
-                s, b, c = chunks[i - 1]
-                if c == 0:
-                    acc = psum_acc.tile([P, P], F32, name="acc")
-                codes, scales = quantised[i - 1]
-                multiply(i - 1, codes, scales, acc)
-                if c == CHUNKS_PER_ROW - 1:
-                    finish(s, b, acc)
+        accs = []
+        for first in range(0, len(chunks), CHUNKS_PER_GROUP):
+            group = range(first, first + CHUNKS_PER_GROUP)
+            s, g = chunks[first][0], chunks[first][1]
+            quantised = []
+            grouped_tiles = []
+            for i in group:
+                if i + X_BUFFERS - 1 < len(chunks):
+                    load_chunk(i + X_BUFFERS - 1)
+                grouped_tiles.append(transpose(i))
+                if i > first:
+                    quantised.append(quantise(grouped_tiles[i - first - 1]))
+            quantised.append(quantise(grouped_tiles[CHUNKS_PER_GROUP - 1]))
+            if g == 0:
+                accs = [psum_acc.tile([P, P], F32, name="acc") for b in range(BATCHES)]
+            for i in group:
+                b, c = chunks[i][2], chunks[i][3]
+                codes, scales = quantised[i - first]
+                multiply(i, codes, scales, accs[b])
+                if g == GROUPS_PER_STREAM - 1 and c == CHUNKS_PER_BATCH - 1:
+                    finish(s, b, accs[b])

import math
from contextlib import ExitStack

import concourse.mybir as mybir
from concourse.masks import make_identity

F32 = mybir.dt.float32
BF16 = mybir.dt.bfloat16
I32 = mybir.dt.int32
U32 = mybir.dt.uint32
U8 = mybir.dt.uint8
FP8X4 = mybir.dt.float8_e4m3fn_x4
ALU = mybir.AluOpType
ACT = mybir.ActivationFunctionType

P = 128
BATCHES = 4
D = 16384
DH = 64
STREAMS = 2
EPS = 1e-12
ROPE_BASE = 10000.0

K_PASS = 4 * P
PASSES = D // K_PASS
PAIRS_PER_PASS = K_PASS // 2
PASSES_PER_CHUNK = 8
CHUNK_COLS = PASSES_PER_CHUNK * K_PASS
PASSES_PER_GROUP = 16
GROUPS_PER_STREAM = PASSES // PASSES_PER_GROUP
CHUNKS_PER_BATCH = PASSES_PER_GROUP // PASSES_PER_CHUNK
CHUNKS_PER_GROUP = BATCHES * CHUNKS_PER_BATCH
PASSES_PER_BANK = 2
BANKS_PER_CHUNK = PASSES_PER_CHUNK // PASSES_PER_BANK
X_BUFFERS = 8

FLOPS = 2 * STREAMS * BATCHES * P * D * P


def tile_cmattention_pb_k_kernel(
    tc, x, a, wx_words, wx_scales, wa_words, wa_scales, kx_scale, ka_scale, k_out, v_out
):
    nc = tc.nc
    acts = (x, a)
    words_in = (wx_words, wa_words)
    scales_in = (wx_scales, wa_scales)
    gains_in = (kx_scale, ka_scale)

    chunks = [
        (s, g, b, c)
        for s in range(STREAMS)
        for g in range(GROUPS_PER_STREAM)
        for b in range(BATCHES)
        for c in range(CHUNKS_PER_BATCH)
    ]

    with ExitStack() as ctx:
        ctx.enter_context(tc.manual_schedule())
        const = ctx.enter_context(tc.tile_pool(name="const", bufs=1))
        x_pool = ctx.enter_context(tc.tile_pool(name="x_pool", bufs=X_BUFFERS))
        stage = ctx.enter_context(tc.tile_pool(name="stage", bufs=3))
        mx_pool = ctx.enter_context(tc.tile_pool(name="mx_pool", bufs=CHUNKS_PER_GROUP))
        small = ctx.enter_context(tc.tile_pool(name="small", bufs=2))
        psum_t = ctx.enter_context(tc.psum_pool(name="psum_t", bufs=4))
        psum_acc = ctx.enter_context(tc.psum_pool(name="psum_acc", bufs=BATCHES))

        w_words = [
            const.tile([P, PASSES, P], U32, name="w_words%d" % s, align_bytes=64)
            for s in range(STREAMS)
        ]
        w_scales = [
            const.tile([P, PASSES, P], U8, name="w_scales%d" % s, align_bytes=64)
            for s in range(STREAMS)
        ]
        for s in range(STREAMS):
            nc.vector.memset(w_scales[s][:].bitcast(I32), 0)

        def load_weight_scales(s):
            for q in range(4):
                nc.sync.dma_start(
                    out=w_scales[s][32 * q : 32 * q + 4].bitcast(I32),
                    in_=scales_in[s][:, 4 * q : 4 * q + 4, :]
                    .rearrange("g r n -> r g n")
                    .bitcast(I32),
                )

        def load_weight_words(s, g):
            passes = slice(g * PASSES_PER_GROUP, (g + 1) * PASSES_PER_GROUP)
            nc.sync.dma_start(
                out=w_words[s][:, passes, :].bitcast(I32),
                in_=words_in[s][passes].rearrange("g p n t -> p g (n t)").bitcast(I32),
            )

        x_tiles = []

        def load_chunk(i):
            s, g, b, c = chunks[i]
            first_col = (g * CHUNKS_PER_BATCH + c) * CHUNK_COLS
            x_sb = x_pool.tile([P, CHUNK_COLS], BF16, name="x_sb")
            nc.sync.dma_start(out=x_sb[:], in_=acts[s][b, :, first_col : first_col + CHUNK_COLS])
            x_tiles.append(x_sb)
            if (i + 1) % CHUNKS_PER_GROUP == 0:
                if g == 0:
                    load_weight_scales(s)
                load_weight_words(s, g)

        for i in range(X_BUFFERS - 1):
            load_chunk(i)

        gains = const.tile([P, STREAMS, DH], BF16, name="gains")
        for s in range(STREAMS):
            nc.scalar.dma_start(
                out=gains[:, s, :],
                in_=gains_in[s].rearrange("a b d -> (a b d)").partition_broadcast(P),
            )

        ident = const.tile([P, P], F32, name="ident")
        make_identity(nc, ident[:])

        turn_offsets = ((0.25, 0.0), (0.5, 0.25))
        col_i = const.tile([P, DH], I32, name="col_i")
        nc.gpsimd.iota(col_i[:], pattern=[[1, DH]], base=0, channel_multiplier=0)
        pos_i = const.tile([P, 1], I32, name="pos_i")
        nc.gpsimd.iota(pos_i[:], pattern=[[0, 1]], base=0, channel_multiplier=1)
        minus_half = const.tile([P, 1], F32, name="minus_half")
        nc.gpsimd.memset(minus_half[:], -0.5)

        col_f = const.tile([P, DH], F32, name="col_f")
        nc.vector.tensor_copy(out=col_f[:], in_=col_i[:])
        pos_turns = const.tile([P, 1], F32, name="pos_turns")
        nc.vector.tensor_scalar_mul(out=pos_turns[:], in0=pos_i[:], scalar1=0.5 / math.pi)
        freq = const.tile([P, DH], F32, name="freq")
        nc.scalar.activation(
            out=freq[:], in_=col_f[:], func=ACT.Exp, scale=-math.log(ROPE_BASE) / DH
        )
        turns = const.tile([P, STREAMS, 2, DH], F32, name="turns")
        for s in range(STREAMS):
            for h in range(2):
                nc.vector.tensor_scalar(
                    out=turns[:, s, h, :],
                    in0=freq[:],
                    scalar1=pos_turns[:, 0:1],
                    scalar2=turn_offsets[s][h],
                    op0=ALU.mult,
                    op1=ALU.add,
                )
        flat = "p s h j -> p (s h j)"
        whole_i = const.tile([P, STREAMS, 2, DH], I32, name="whole_i")
        nc.vector.tensor_copy(out=whole_i[:], in_=turns[:])
        whole_f = const.tile([P, STREAMS, 2, DH], F32, name="whole_f")
        nc.vector.tensor_copy(out=whole_f[:], in_=whole_i[:])
        left = const.tile([P, STREAMS, 2, DH], F32, name="left")
        nc.vector.tensor_sub(out=left[:], in0=turns[:], in1=whole_f[:])
        minus_turn = const.tile([P, STREAMS, 2, DH], F32, name="minus_turn")
        nc.vector.scalar_tensor_tensor(
            out=minus_turn[:].rearrange(flat),
            in0=left[:].rearrange(flat),
            scalar=0.5,
            in1=left[:].rearrange(flat),
            op0=ALU.is_gt,
            op1=ALU.subtract,
        )
        trig = const.tile([P, STREAMS, 2, DH], F32, name="trig")
        nc.scalar.activation(
            out=trig[:], in_=minus_turn[:], func=ACT.Sin, scale=-2.0 * math.pi
        )
        table = const.tile([P, STREAMS, 2, DH], F32, name="table")
        nc.vector.tensor_tensor(
            out=table[:],
            in0=trig[:],
            in1=gains[:].unsqueeze(2).to_broadcast([P, STREAMS, 2, DH]),
            op=ALU.mult,
        )

        k_from_x = [const.tile([P, 2, DH], F32, name="k_from_x%d" % b) for b in range(BATCHES)]
        v_sb = [const.tile([P, STREAMS, DH], F32, name="v_sb%d" % b) for b in range(BATCHES)]

        def transpose(i):
            pairs = x_tiles[i][:].bitcast(F32)
            grouped = stage.tile([P, CHUNK_COLS], BF16, name="grouped", align_bytes=64)
            grouped_pairs = grouped[:].bitcast(F32).rearrange("p (g r u) -> p g r u", r=P, u=2)
            for h in range(BANKS_PER_CHUNK):
                bank = psum_t.tile([P, PASSES_PER_BANK, 2, P], F32, name="bank")
                for j in range(PASSES_PER_BANK):
                    first = (h * PASSES_PER_BANK + j) * PAIRS_PER_PASS
                    for u in range(2):
                        nc.tensor.transpose(
                            bank[:, j, u, :],
                            pairs[:, first + u : first + PAIRS_PER_PASS : 2],
                            ident[:],
                        )
                copy_out = nc.vector.tensor_copy if h == 0 else nc.scalar.copy
                copy_out(
                    out=grouped_pairs[:, h * PASSES_PER_BANK : (h + 1) * PASSES_PER_BANK],
                    in_=bank[:].rearrange("p j u r -> p j r u"),
                )
            return grouped

        def quantise(grouped):
            codes = mx_pool.tile([P, PASSES_PER_CHUNK * P], U32, name="codes", align_bytes=64)
            scales = mx_pool.tile([P, PASSES_PER_CHUNK * P], U8, name="scales", align_bytes=64)
            nc.vector.quantize_mx(out=codes[:].bitcast(FP8X4), scales=scales[:], in_=grouped[:])
            return codes, scales

        def multiply(i, codes, scales, acc):
            s, g, b, c = chunks[i]
            for j in range(PASSES_PER_CHUNK):
                k_pass = g * PASSES_PER_GROUP + c * PASSES_PER_CHUNK + j
                tokens = slice(j * P, (j + 1) * P)
                nc.tensor.matmul_mx(
                    out=acc[:],
                    lhsT=codes[:, tokens].bitcast(FP8X4),
                    lhsT_scale=scales[:, tokens],
                    rhs=w_words[s][:, k_pass, :].bitcast(FP8X4),
                    rhs_scale=w_scales[s][:, k_pass, :],
                    start=(k_pass == 0),
                    stop=(k_pass == PASSES - 1),
                )

        def finish(s, b, acc):
            nc.scalar.copy(out=v_sb[b][:, s, :], in_=acc[:, DH : 2 * DH])
            squares = small.tile([P, DH], F32, name="squares")
            sum_sq = small.tile([P, 1], F32, name="sum_sq")
            nc.scalar.activation(
                out=squares[:], in_=acc[:, 0:DH], func=ACT.Square, accum_out=sum_sq[:]
            )
            floored = small.tile([P, 1], F32, name="floored")
            nc.gpsimd.tensor_scalar_max(out=floored[:], in0=sum_sq[:], scalar1=EPS * EPS)
            inv_norm = small.tile([P, 1], F32, name="inv_norm")
            nc.gpsimd.tensor_tensor(
                out=inv_norm[:], in0=floored[:], in1=minus_half[:], op=ALU.pow
            )
            share = k_from_x[b] if s == 0 else small.tile([P, 2, DH], F32, name="k_from_a")
            nc.vector.scalar_tensor_tensor(
                out=share[:],
                in0=acc[:, 0:DH].unsqueeze(1).to_broadcast([P, 2, DH]),
                scalar=inv_norm[:, 0:1],
                in1=table[:, s],
                op0=ALU.mult,
                op1=ALU.mult,
            )
            if s == STREAMS - 1:
                k_sb = small.tile([P, 2, DH], F32, name="k_sb")
                nc.vector.tensor_add(out=k_sb[:], in0=k_from_x[b][:], in1=share[:])
                nc.sync.dma_start(out=v_out[b], in_=v_sb[b][:].rearrange("p s j -> p (s j)"))
                nc.sync.dma_start(out=k_out[b], in_=k_sb[:].rearrange("p h j -> p (h j)"))

        accs = []
        for first in range(0, len(chunks), CHUNKS_PER_GROUP):
            group = range(first, first + CHUNKS_PER_GROUP)
            s, g = chunks[first][0], chunks[first][1]
            quantised = []
            grouped_tiles = []
            for i in group:
                if i + X_BUFFERS - 1 < len(chunks):
                    load_chunk(i + X_BUFFERS - 1)
                grouped_tiles.append(transpose(i))
                if i > first:
                    quantised.append(quantise(grouped_tiles[i - first - 1]))
            quantised.append(quantise(grouped_tiles[CHUNKS_PER_GROUP - 1]))
            if g == 0:
                accs = [psum_acc.tile([P, P], F32, name="acc") for b in range(BATCHES)]
            for i in group:
                b, c = chunks[i][2], chunks[i][3]
                codes, scales = quantised[i - first]
                multiply(i, codes, scales, accs[b])
                if g == GROUPS_PER_STREAM - 1 and c == CHUNKS_PER_BATCH - 1:
                    finish(s, b, accs[b])
